import numpy as np
import ml_dtypes


def mxq(x, axis, fmt="e4m3"):
    dtype, down = {"e4m3": (ml_dtypes.float8_e4m3fn, 7), "e5m2": (ml_dtypes.float8_e5m2, 14)}[fmt]
    v = np.moveaxis(np.asarray(x, np.float32).astype(ml_dtypes.bfloat16).astype(np.float64), axis, -1)
    blocks = v.reshape(v.shape[:-1] + (-1, 32))
    amax = np.abs(blocks).max(-1, keepdims=True)
    byte = np.maximum(np.where(amax > 0, np.frexp(amax)[1] - 1 + 127, 0) - down, 1)
    scale = np.exp2(byte - 127.0)
    codes = (blocks / scale).astype(np.float32).astype(dtype).astype(np.float64)
    return np.moveaxis((codes * scale).reshape(v.shape), -1, axis)


WIDE = False


def mx_kscale(k):
    if not WIDE:
        return np.ones(k)
    levels = np.array([10, -10, 5, -5, 0])
    if k % 512:
        return np.exp2(np.random.permutation(np.resize(levels, k // 32))).repeat(32)
    a = np.empty((k // 512, 16))
    for p in range(k // 512):
        a[p, :8] = np.random.permutation(np.resize(levels, 8))
        for g in range(8):
            far = levels[np.abs(levels - a[p, g]) >= 10]
            a[p, g + 8] = far[np.random.randint(len(far))]
    return np.exp2(a.ravel()).repeat(32)


BF16 = ml_dtypes.bfloat16


def bf(x):
    return np.asarray(x, np.float32).astype(BF16)


def f64(x):
    return np.asarray(x).astype(np.float64)


B, D_IN, D_H = 512, 1024, 1024


def sigmoid(v):
    return 1.0 / (1.0 + np.exp(-v))


def setup_inputs():
    s, t = mx_kscale(D_IN), mx_kscale(D_H)
    fg = np.exp(0.75 * np.random.standard_normal((B, D_H)))
    ig = np.exp(0.75 * np.random.standard_normal((B, D_H)))
    c = fg * np.random.standard_normal((B, D_H)) + ig * np.tanh(0.75 * np.random.standard_normal((B, D_H)))
    n = fg * np.random.uniform(size=(B, D_H)) + ig
    return {"x": bf(np.random.standard_normal((B, D_IN)) * s),
            "h_prev": bf(np.random.standard_normal((B, D_H)) * t),
            "c": bf(c),
            "n": bf(n),
            "W_o": bf(np.random.standard_normal((D_IN, D_H)) * 0.5 / np.sqrt(D_IN) / s[:, None]),
            "b_o": bf(np.random.standard_normal(D_H) * 0.3),
            "U_o": bf(np.random.standard_normal((D_H, D_H)) * 0.5 / np.sqrt(D_H) / t[:, None])}


def core(x, h_prev, c, n, W_o, b_o, U_o):
    o = sigmoid((mxq(f64(x), 1, "e4m3") @ mxq(f64(W_o), 0, "e4m3")) + f64(b_o) + (mxq(f64(h_prev), 1, "e4m3") @ mxq(f64(U_o), 0, "e4m3")))
    return o * (f64(c) / (f64(n) + 1e-6))


def e4m3fn_bytes(y):
    return np.clip(np.asarray(y, np.float64), -448.0, 448.0).astype(np.float32).astype(ml_dtypes.float8_e4m3fn).view(np.uint8)


def reference(x, h_prev, c, n, W_o, b_o, U_o):
    out = core(x, h_prev, c, n, W_o, b_o, U_o)
    s = np.max(np.abs(out), axis=-1, keepdims=True) / 448.0
    return out, e4m3fn_bytes(out / s)

@@ -1,0 +1,296 @@
+from contextlib import ExitStack
+
+import concourse.mybir as mybir
+from concourse.masks import make_identity
+
+B, D_IN, D_H = 512, 1024, 1024
+FLOPS = 2 * B * (D_IN + D_H) * D_H
+
+F32 = mybir.dt.float32
+BF16 = mybir.dt.bfloat16
+U32 = mybir.dt.uint32
+U8 = mybir.dt.uint8
+FP8X4 = mybir.dt.float8_e4m3fn_x4
+FP8 = mybir.dt.float8_e4m3fn
+ACT = mybir.ActivationFunctionType
+ALU = mybir.AluOpType
+AX = mybir.AxisListType
+
+P = 128
+RT = B // P
+NPASS = 4
+HALF = 512
+HROW = D_H + 8
+
+
+def tile_slstmcell_pb_kernel(tc, x, h_prev, c, n, W_o, b_o, U_o, out_0, out_1):
+    nc = tc.nc
+    with ExitStack() as ctx:
+        keep = ctx.enter_context(tc.tile_pool(name="keep", bufs=1))
+        wgp = ctx.enter_context(tc.tile_pool(name="wgp", bufs=4))
+        psum = ctx.enter_context(tc.psum_pool(name="psum", bufs=1))
+        ctx.enter_context(tc.manual_schedule())
+
+        def bank(name, shape, dtype, tag):
+            return psum.tile(shape, dtype, name=name, tag=tag)
+
+        w_raw = [keep.tile([P, 4, D_H], BF16, name="w_raw_%d" % g) for g in range(NPASS)]
+        x_sb = [keep.tile([P, RT, 1024], BF16, name="x_sb"), keep.tile([P, RT, 1024], BF16, name="h_sb")]
+        n_sb = keep.tile([P, RT, D_H], BF16, name="n_sb")
+        c_sb = keep.tile([P, RT, D_H], BF16, name="c_sb")
+        wq = keep.tile([P, NPASS, D_H], U32, name="wq", align_bytes=64)
+        ws = keep.tile([P, NPASS, D_H], U8, name="ws", align_bytes=64)
+        xq = keep.tile([P, NPASS, B], U32, name="xq", align_bytes=64)
+        xs = keep.tile([P, NPASS, B], U8, name="xs", align_bytes=64)
+        xg = [keep.tile([P, B, 4], BF16, name="xg_%d" % g, align_bytes=64) for g in range(NPASS)]
+        rq = keep.tile([P, RT, D_H], F32, name="rq")
+        h_all = keep.tile([P, RT, HROW], F32, name="h_all")
+        am = keep.tile([P, RT], F32, name="am")
+        ra = keep.tile([P, RT], F32, name="ra")
+        sc = keep.tile([P, RT], F32, name="sc")
+        o8 = [keep.tile([P, D_H], FP8, name="o8_%d" % t) for t in range(RT)]
+        ot = {}
+        for s in range(2):
+            for k in range(4):
+                ot[(s, k)] = keep.tile([P, B], F32, name="ot_%d_%d" % (s, k))
+        ident = keep.tile([P, P], F32, name="ident")
+        identb = keep.tile([P, P], BF16, name="identb")
+        b_rows = keep.tile([P, P], BF16, name="b_rows")
+        b_sb = keep.tile([P, 8], F32, name="b_sb")
+        zero = keep.tile([P, 1], F32, name="zero")
+        one = keep.tile([P, 1], F32, name="one")
+        warm = keep.tile([P, 2], F32, name="warm")
+        hold = keep.tile([P, 1], F32, name="hold")
+
+        out0_v = out_0.rearrange("(p t) m -> p t m", t=RT)
+        out1_v = out_1.rearrange("(p t) m -> p t m", t=RT)
+
+        def load_w(g):
+            src = W_o if g < 2 else U_o
+            k0 = 512 * (g % 2)
+            nc.sync.dma_start(out=w_raw[g][:], in_=src[k0 : k0 + 512, :].rearrange("(p j) m -> p j m", j=4))
+
+        def load_rows(dst, src, t0, t1):
+            nc.sync.dma_start(out=dst[:, t0:t1, :], in_=src.rearrange("(p t) k -> p t k", t=RT)[:, t0:t1, :])
+
+        load_w(0)
+        load_rows(n_sb, n, 0, 2)
+        load_w(1)
+        load_rows(x_sb[0], x, 0, 4)
+        load_rows(x_sb[1], h_prev, 0, 4)
+        load_w(2)
+        load_rows(n_sb, n, 2, 4)
+        load_w(3)
+        load_rows(c_sb, c, 0, 4)
+
+        nc.gpsimd.memset(b_rows[:], 0.0)
+        make_identity(nc, identb[:])
+        make_identity(nc, ident[:])
+        nc.vector.memset(one[:], 1.0)
+        nc.vector.memset(zero[:], 0.0)
+        nc.scalar.dma_start(out=b_rows[0:8, :], in_=b_o.rearrange("(t p) -> t p", p=P))
+        nc.scalar.activation(out=warm[:, 0:1], in_=one[:], func=ACT.Abs_reciprocal_sqrt)
+        b_t = bank("b_t", [P, P], BF16, "A3")
+        nc.tensor.transpose(b_t[:], b_rows[:], identb[:])
+
+        wg = {}
+
+        def interleave(g, s, s_cols):
+            t = wgp.tile([P, HALF, 4], BF16, name="wg_%d_%d" % (g, s), tag="wg", align_bytes=64)
+            wg[(g, s)] = t
+            a = HALF - s_cols
+            src = w_raw[g][:, :, HALF * s : HALF * (s + 1)]
+            if a > 0:
+                nc.vector.tensor_copy(
+                    out=t[:, 0:a, :].rearrange("p (q i) j -> p q j i", i=4), in_=src[:, :, 0:a].rearrange("p j (q i) -> p q j i", i=4)
+                )
+            if s_cols > 0:
+                nc.scalar.copy(
+                    out=t[:, a:HALF, :].rearrange("p (q i) j -> p q j i", i=4),
+                    in_=src[:, :, a:HALF].rearrange("p j (q i) -> p q j i", i=4),
+                )
+
+        def quant_w(g, s):
+            cols = slice(HALF * s, HALF * (s + 1))
+            nc.vector.quantize_mx(
+                out=wq[:, g, cols].bitcast(FP8X4), scales=ws[:, g, cols], in_=wg[(g, s)][:].rearrange("p m j -> p (m j)")
+            )
+
+        def rsqrt_n(t):
+            nc.scalar.activation(out=rq[:, t, :], in_=n_sb[:, t, :], func=ACT.Abs_reciprocal_sqrt, bias=1e-6, scale=1.0)
+
+        def square_n(t):
+            nc.scalar.activation(out=rq[:, t, :], in_=rq[:, t, :], func=ACT.Square)
+
+        def ratio(eng, t, s):
+            cols = slice(HALF * s, HALF * (s + 1))
+            eng.tensor_tensor(out=rq[:, t, cols], in0=c_sb[:, t, cols], in1=rq[:, t, cols], op=ALU.mult)
+
+        def turn_x(g):
+            src = x_sb[g // 2]
+            gl = g % 2
+            words_out = xg[g][:].rearrange("p r t -> p (r t)").bitcast(F32).rearrange("p (a r u) -> p a r u", a=RT, u=2)
+            for pair in range(2):
+                tr = bank("tr_%d_%d" % (g, pair), [P, 2, 2, P], F32, "B%d" % ((2 * g + pair) % 4))
+                for a in range(2):
+                    words = src[:, 2 * pair + a, :].bitcast(F32)
+                    for u in range(2):
+                        nc.tensor.transpose(tr[:, a, u, :], words[:, 256 * gl + u : 256 * (gl + 1) : 2], ident[:])
+                nc.scalar.copy(out=words_out[:, 2 * pair : 2 * pair + 2, :, :], in_=tr[:].rearrange("p a u r -> p a r u"))
+
+        def quant_x(g):
+            nc.vector.quantize_mx(out=xq[:, g, :].bitcast(FP8X4), scales=xs[:, g, :], in_=xg[g][:].rearrange("p r t -> p (r t)"))
+
+        acc = {}
+
+        def mx(s, g):
+            for k in range(4):
+                if g == 0:
+                    acc[(s, k)] = bank("acc_%d_%d" % (s, k), [P, B], F32, "%s%d" % ("AB"[s], k))
+                ch = slice(HALF * s + P * k, HALF * s + P * (k + 1))
+                nc.tensor.matmul_mx(
+                    out=acc[(s, k)][:],
+                    lhsT=wq[:, g, ch].bitcast(FP8X4),
+                    lhsT_scale=ws[:, g, ch],
+                    rhs=xq[:, g, :].bitcast(FP8X4),
+                    rhs_scale=xs[:, g, :],
+                    start=(g == 0),
+                    stop=(g == NPASS - 1),
+                )
+
+        def gate(s):
+            for k in range(4):
+                nc.scalar.activation(
+                    out=ot[(s, k)][:], in_=acc[(s, k)][:], func=ACT.Sigmoid, bias=b_sb[:, 4 * s + k : 4 * s + k + 1], scale=1.0
+                )
+
+        ob = {}
+
+        def back(s, t):
+            ob[(s, t)] = bank("ob_%d_%d" % (s, t), [P, HALF], F32, "%s%d" % ("AB"[s], t))
+            for k in range(4):
+                nc.tensor.transpose(ob[(s, t)][:, P * k : P * (k + 1)], ot[(s, k)][:, P * t : P * (t + 1)], ident[:])
+
+        def prod(s, t):
+            cols = slice(HALF * s, HALF * (s + 1))
+            nc.vector.tensor_tensor(out=h_all[:, t, cols], in0=ob[(s, t)][:], in1=rq[:, t, cols], op=ALU.mult)
+            nc.sync.dma_start(out=out0_v[:, t, cols], in_=h_all[:, t, cols])
+
+        def amax(s, t):
+            if s == 0:
+                nc.vector.tensor_reduce(
+                    out=h_all[:, t, D_H : D_H + 1], in_=h_all[:, t, 0:HALF], axis=AX.X, op=ALU.max, apply_absolute_value=True
+                )
+            else:
+                nc.vector.tensor_reduce(
+                    out=am[:, t : t + 1], in_=h_all[:, t, HALF : D_H + 1], axis=AX.X, op=ALU.max, apply_absolute_value=True
+                )
+
+        def recip(t):
+            nc.vector.reciprocal(out=ra[:, t : t + 1], in_=am[:, t : t + 1])
+
+        def cast_s(t, v_cols):
+            nc.scalar.activation(out=sc[:, t : t + 1], in_=ra[:, t : t + 1], func=ACT.Copy, scale=448.0)
+            a = D_H - v_cols
+            nc.scalar.activation(
+                out=o8[t][:, 0:a], in_=h_all[:, t, 0:a], func=ACT.Identity, scale=sc[:, t : t + 1], bias=zero[:, 0:1], saturate=False
+            )
+
+        def cast_v(t, v_cols):
+            a = D_H - v_cols
+            nc.vector.tensor_scalar(
+                out=o8[t][:, a:D_H], in0=h_all[:, t, a:D_H], scalar1=sc[:, t : t + 1], scalar2=None, op0=ALU.mult, saturate=False
+            )
+
+        def store8(t):
+            nc.sync.dma_start(out=out1_v[:, t, :], in_=o8[t][:].bitcast(U8))
+
+        interleave(0, 0, 0)
+        interleave(0, 1, 256)
+        quant_w(0, 0)
+        quant_w(0, 1)
+        rsqrt_n(0)
+        rsqrt_n(1)
+        square_n(0)
+        square_n(1)
+        nc.scalar.copy(out=b_sb[:], in_=b_t[:, 0:8])
+        interleave(1, 0, 0)
+        interleave(1, 1, 0)
+        quant_w(1, 0)
+        quant_w(1, 1)
+        for g in range(NPASS):
+            turn_x(g)
+        quant_x(0)
+        quant_x(1)
+        mx(0, 0)
+        mx(0, 1)
+        mx(1, 0)
+        mx(1, 1)
+        quant_x(2)
+        interleave(2, 0, 0)
+        quant_x(3)
+        interleave(2, 1, 0)
+        interleave(3, 0, 0)
+        quant_w(2, 0)
+        quant_w(3, 0)
+        rsqrt_n(2)
+        rsqrt_n(3)
+        nc.scalar.activation(out=warm[:, 1:2], in_=one[:], func=ACT.Sigmoid)
+        interleave(3, 1, HALF)
+        mx(0, 2)
+        mx(0, 3)
+        quant_w(2, 1)
+        ratio(nc.vector, 0, 0)
+        ratio(nc.vector, 1, 0)
+        quant_w(3, 1)
+        ratio(nc.vector, 0, 1)
+        ratio(nc.vector, 1, 1)
+        mx(1, 2)
+        gate(0)
+        square_n(2)
+        nc.gpsimd.tensor_copy(out=hold[:], in_=rq[:, 1, HALF : HALF + 1])
+        ratio(nc.gpsimd, 2, 0)
+        ratio(nc.gpsimd, 2, 1)
+        back(0, 0)
+        back(0, 1)
+        mx(1, 3)
+        back(0, 2)
+        prod(0, 0)
+        prod(0, 1)
+        amax(0, 0)
+        prod(0, 2)
+        amax(0, 1)
+        gate(1)
+        square_n(3)
+        ratio(nc.gpsimd, 3, 0)
+        ratio(nc.gpsimd, 3, 1)
+        back(1, 0)
+        back(1, 1)
+        back(1, 2)
+        back(0, 3)
+        back(1, 3)
+        prod(1, 0)
+        amax(0, 2)
+        prod(1, 1)
+        amax(1, 0)
+        prod(1, 2)
+        amax(1, 1)
+        recip(0)
+        prod(0, 3)
+        cast_s(0, 0)
+        store8(0)
+        amax(1, 2)
+        recip(1)
+        prod(1, 3)
+        cast_s(1, 0)
+        store8(1)
+        amax(0, 3)
+        recip(2)
+        amax(1, 3)
+        recip(3)
+        cast_s(2, 384)
+        cast_v(2, 384)
+        store8(2)
+        cast_s(3, 704)
+        cast_v(3, 704)
+        store8(3)

@@ -116,8 +116,8 @@ def tile_slstmcell_pb_kernel(tc, x, h_prev, c, n, W_o, b_o, U_o, out_0, out_1):
                 out=wq[:, g, cols].bitcast(FP8X4), scales=ws[:, g, cols], in_=wg[(g, s)][:].rearrange("p m j -> p (m j)")
             )
 
-        def rsqrt_n(t):
-            nc.scalar.activation(out=rq[:, t, :], in_=n_sb[:, t, :], func=ACT.Abs_reciprocal_sqrt, bias=1e-6, scale=1.0)
+        def rsqrt_n(t0, t1):
+            nc.scalar.activation(out=rq[:, t0:t1, :], in_=n_sb[:, t0:t1, :], func=ACT.Abs_reciprocal_sqrt, bias=1e-6, scale=1.0)
 
         def square_n(t):
             nc.scalar.activation(out=rq[:, t, :], in_=rq[:, t, :], func=ACT.Square)
@@ -126,7 +126,7 @@ def tile_slstmcell_pb_kernel(tc, x, h_prev, c, n, W_o, b_o, U_o, out_0, out_1):
             cols = slice(HALF * s, HALF * (s + 1))
             eng.tensor_tensor(out=rq[:, t, cols], in0=c_sb[:, t, cols], in1=rq[:, t, cols], op=ALU.mult)
 
-        def turn_x(g):
+        def turn_x(g, on_vector=False):
             src = x_sb[g // 2]
             gl = g % 2
             words_out = xg[g][:].rearrange("p r t -> p (r t)").bitcast(F32).rearrange("p (a r u) -> p a r u", a=RT, u=2)
@@ -136,7 +136,10 @@ def tile_slstmcell_pb_kernel(tc, x, h_prev, c, n, W_o, b_o, U_o, out_0, out_1):
                     words = src[:, 2 * pair + a, :].bitcast(F32)
                     for u in range(2):
                         nc.tensor.transpose(tr[:, a, u, :], words[:, 256 * gl + u : 256 * (gl + 1) : 2], ident[:])
-                nc.scalar.copy(out=words_out[:, 2 * pair : 2 * pair + 2, :, :], in_=tr[:].rearrange("p a u r -> p a r u"))
+                if on_vector:
+                    nc.vector.tensor_copy(out=words_out[:, 2 * pair : 2 * pair + 2, :, :], in_=tr[:].rearrange("p a u r -> p a r u"))
+                else:
+                    nc.scalar.copy(out=words_out[:, 2 * pair : 2 * pair + 2, :, :], in_=tr[:].rearrange("p a u r -> p a r u"))
 
         def quant_x(g):
             nc.vector.quantize_mx(out=xq[:, g, :].bitcast(FP8X4), scales=xs[:, g, :], in_=xg[g][:].rearrange("p r t -> p (r t)"))
@@ -209,8 +212,8 @@ def tile_slstmcell_pb_kernel(tc, x, h_prev, c, n, W_o, b_o, U_o, out_0, out_1):
         interleave(0, 1, 256)
         quant_w(0, 0)
         quant_w(0, 1)
-        rsqrt_n(0)
-        rsqrt_n(1)
+        rsqrt_n(0, 1)
+        rsqrt_n(1, 2)
         square_n(0)
         square_n(1)
         nc.scalar.copy(out=b_sb[:], in_=b_t[:, 0:8])
@@ -218,38 +221,39 @@ def tile_slstmcell_pb_kernel(tc, x, h_prev, c, n, W_o, b_o, U_o, out_0, out_1):
         interleave(1, 1, 0)
         quant_w(1, 0)
         quant_w(1, 1)
-        for g in range(NPASS):
-            turn_x(g)
+        turn_x(0)
+        turn_x(1)
+        turn_x(2)
         quant_x(0)
         quant_x(1)
+        turn_x(3, on_vector=True)
         mx(0, 0)
         mx(0, 1)
         mx(1, 0)
         mx(1, 1)
-        quant_x(2)
         interleave(2, 0, 0)
-        quant_x(3)
-        interleave(2, 1, 0)
-        interleave(3, 0, 0)
+        interleave(2, 1, HALF)
+        quant_x(2)
         quant_w(2, 0)
-        quant_w(3, 0)
-        rsqrt_n(2)
-        rsqrt_n(3)
+        rsqrt_n(2, 4)
         nc.scalar.activation(out=warm[:, 1:2], in_=one[:], func=ACT.Sigmoid)
-        interleave(3, 1, HALF)
         mx(0, 2)
+        interleave(3, 0, 0)
+        quant_x(3)
+        quant_w(3, 0)
         mx(0, 3)
         quant_w(2, 1)
-        ratio(nc.vector, 0, 0)
-        ratio(nc.vector, 1, 0)
-        quant_w(3, 1)
-        ratio(nc.vector, 0, 1)
-        ratio(nc.vector, 1, 1)
         mx(1, 2)
+        interleave(3, 1, 0)
+        ratio(nc.vector, 0, 0)
+        quant_w(3, 1)
+        ratio(nc.vector, 1, 0)
+        ratio(nc.vector, 0, 1)
         gate(0)
         square_n(2)
-        nc.gpsimd.tensor_copy(out=hold[:], in_=rq[:, 1, HALF : HALF + 1])
+        nc.gpsimd.tensor_copy(out=hold[:], in_=rq[:, 0, HALF : HALF + 1])
         ratio(nc.gpsimd, 2, 0)
+        ratio(nc.gpsimd, 1, 1)
         ratio(nc.gpsimd, 2, 1)
         back(0, 0)
         back(0, 1)
@@ -258,7 +262,6 @@ def tile_slstmcell_pb_kernel(tc, x, h_prev, c, n, W_o, b_o, U_o, out_0, out_1):
         prod(0, 0)
         prod(0, 1)
         amax(0, 0)
-        prod(0, 2)
         amax(0, 1)
         gate(1)
         square_n(3)
@@ -269,28 +272,28 @@ def tile_slstmcell_pb_kernel(tc, x, h_prev, c, n, W_o, b_o, U_o, out_0, out_1):
         back(1, 2)
         back(0, 3)
         back(1, 3)
+        prod(0, 2)
         prod(1, 0)
         amax(0, 2)
         prod(1, 1)
         amax(1, 0)
         prod(1, 2)
-        amax(1, 1)
         recip(0)
-        prod(0, 3)
         cast_s(0, 0)
         store8(0)
-        amax(1, 2)
+        amax(1, 1)
+        prod(0, 3)
         recip(1)
-        prod(1, 3)
         cast_s(1, 0)
         store8(1)
-        amax(0, 3)
+        amax(1, 2)
+        prod(1, 3)
         recip(2)
+        cast_s(2, 0)
+        store8(2)
+        amax(0, 3)
         amax(1, 3)
         recip(3)
-        cast_s(2, 384)
-        cast_v(2, 384)
-        store8(2)
-        cast_s(3, 704)
-        cast_v(3, 704)
+        cast_s(3, 640)
+        cast_v(3, 640)
         store8(3)

@@ -61,6 +61,7 @@ def tile_slstmcell_pb_kernel(tc, x, h_prev, c, n, W_o, b_o, U_o, out_0, out_1):
         one = keep.tile([P, 1], F32, name="one")
         warm = keep.tile([P, 2], F32, name="warm")
         hold = keep.tile([P, 1], F32, name="hold")
+        oc = keep.tile([P, HALF], F32, name="oc")
 
         out0_v = out_0.rearrange("(p t) m -> p t m", t=RT)
         out1_v = out_1.rearrange("(p t) m -> p t m", t=RT)
@@ -179,6 +180,14 @@ def tile_slstmcell_pb_kernel(tc, x, h_prev, c, n, W_o, b_o, U_o, out_0, out_1):
             nc.vector.tensor_tensor(out=h_all[:, t, cols], in0=ob[(s, t)][:], in1=rq[:, t, cols], op=ALU.mult)
             nc.sync.dma_start(out=out0_v[:, t, cols], in_=h_all[:, t, cols])
 
+        def o_copy(s, t):
+            nc.scalar.copy(out=oc[:], in_=ob[(s, t)][:])
+
+        def prod_g(s, t):
+            cols = slice(HALF * s, HALF * (s + 1))
+            nc.gpsimd.tensor_tensor(out=h_all[:, t, cols], in0=oc[:], in1=rq[:, t, cols], op=ALU.mult)
+            nc.sync.dma_start(out=out0_v[:, t, cols], in_=h_all[:, t, cols])
+
         def amax(s, t):
             if s == 0:
                 nc.vector.tensor_reduce(
@@ -272,6 +281,7 @@ def tile_slstmcell_pb_kernel(tc, x, h_prev, c, n, W_o, b_o, U_o, out_0, out_1):
         back(1, 2)
         back(0, 3)
         back(1, 3)
+        o_copy(1, 3)
         prod(0, 2)
         prod(1, 0)
         amax(0, 2)
@@ -287,12 +297,13 @@ def tile_slstmcell_pb_kernel(tc, x, h_prev, c, n, W_o, b_o, U_o, out_0, out_1):
         cast_s(1, 0)
         store8(1)
         amax(1, 2)
-        prod(1, 3)
-        recip(2)
-        cast_s(2, 0)
-        store8(2)
+        prod_g(1, 3)
         amax(0, 3)
+        recip(2)
+        cast_s(2, 512)
         amax(1, 3)
+        cast_v(2, 512)
+        store8(2)
         recip(3)
         cast_s(3, 640)
         cast_v(3, 640)

@@ -96,6 +96,20 @@ def tile_slstmcell_pb_kernel(tc, x, h_prev, c, n, W_o, b_o, U_o, out_0, out_1):
 
         wg = {}
 
+        def interleave_part(g, s, lo, hi):
+            if lo == 0:
+                wg[(g, s)] = wgp.tile([P, HALF, 4], BF16, name="wg_%d_%d" % (g, s), tag="wg", align_bytes=64)
+            nc.vector.tensor_copy(
+                out=wg[(g, s)][:, lo:hi, :].rearrange("p (q i) j -> p q j i", i=4),
+                in_=w_raw[g][:, :, HALF * s + lo : HALF * s + hi].rearrange("p j (q i) -> p q j i", i=4),
+            )
+
+        def quant_part(g, s, lo, hi):
+            cols = slice(HALF * s + lo, HALF * s + hi)
+            nc.vector.quantize_mx(
+                out=wq[:, g, cols].bitcast(FP8X4), scales=ws[:, g, cols], in_=wg[(g, s)][:, lo:hi, :].rearrange("p m j -> p (m j)")
+            )
+
         def interleave(g, s, s_cols):
             t = wgp.tile([P, HALF, 4], BF16, name="wg_%d_%d" % (g, s), tag="wg", align_bytes=64)
             wg[(g, s)] = t
@@ -247,9 +261,11 @@ def tile_slstmcell_pb_kernel(tc, x, h_prev, c, n, W_o, b_o, U_o, out_0, out_1):
         rsqrt_n(2, 4)
         nc.scalar.activation(out=warm[:, 1:2], in_=one[:], func=ACT.Sigmoid)
         mx(0, 2)
-        interleave(3, 0, 0)
         quant_x(3)
-        quant_w(3, 0)
+        interleave_part(3, 0, 0, 256)
+        interleave_part(3, 0, 256, HALF)
+        quant_part(3, 0, 0, 256)
+        quant_part(3, 0, 256, HALF)
         mx(0, 3)
         quant_w(2, 1)
         mx(1, 2)

@@ -79,8 +79,8 @@ def tile_slstmcell_pb_kernel(tc, x, h_prev, c, n, W_o, b_o, U_o, out_0, out_1):
         load_w(1)
         load_rows(x_sb[0], x, 0, 4)
         load_rows(x_sb[1], h_prev, 0, 4)
-        load_w(2)
         load_rows(n_sb, n, 2, 4)
+        load_w(2)
         load_w(3)
         load_rows(c_sb, c, 0, 4)
 
@@ -254,18 +254,22 @@ def tile_slstmcell_pb_kernel(tc, x, h_prev, c, n, W_o, b_o, U_o, out_0, out_1):
         mx(0, 1)
         mx(1, 0)
         mx(1, 1)
+        rsqrt_n(2, 4)
+        quant_x(2)
+        quant_x(3)
         interleave(2, 0, 0)
         interleave(2, 1, HALF)
-        quant_x(2)
-        quant_w(2, 0)
-        rsqrt_n(2, 4)
         nc.scalar.activation(out=warm[:, 1:2], in_=one[:], func=ACT.Sigmoid)
+        quant_w(2, 0)
         mx(0, 2)
-        quant_x(3)
-        interleave_part(3, 0, 0, 256)
-        interleave_part(3, 0, 256, HALF)
-        quant_part(3, 0, 0, 256)
-        quant_part(3, 0, 256, HALF)
+        interleave_part(3, 0, 0, 128)
+        interleave_part(3, 0, 128, 256)
+        quant_part(3, 0, 0, 128)
+        interleave_part(3, 0, 256, 384)
+        quant_part(3, 0, 128, 256)
+        interleave_part(3, 0, 384, HALF)
+        quant_part(3, 0, 256, 384)
+        quant_part(3, 0, 384, HALF)
         mx(0, 3)
         quant_w(2, 1)
         mx(1, 2)

@@ -77,8 +77,10 @@ def tile_slstmcell_pb_kernel(tc, x, h_prev, c, n, W_o, b_o, U_o, out_0, out_1):
         load_w(0)
         load_rows(n_sb, n, 0, 2)
         load_w(1)
-        load_rows(x_sb[0], x, 0, 4)
-        load_rows(x_sb[1], h_prev, 0, 4)
+        load_rows(x_sb[0], x, 0, 2)
+        load_rows(x_sb[0], x, 2, 4)
+        load_rows(x_sb[1], h_prev, 0, 2)
+        load_rows(x_sb[1], h_prev, 2, 4)
         load_rows(n_sb, n, 2, 4)
         load_w(2)
         load_w(3)
@@ -141,11 +143,11 @@ def tile_slstmcell_pb_kernel(tc, x, h_prev, c, n, W_o, b_o, U_o, out_0, out_1):
             cols = slice(HALF * s, HALF * (s + 1))
             eng.tensor_tensor(out=rq[:, t, cols], in0=c_sb[:, t, cols], in1=rq[:, t, cols], op=ALU.mult)
 
-        def turn_x(g, on_vector=False):
+        def turn_x(g, pair, on_vector=False):
             src = x_sb[g // 2]
             gl = g % 2
             words_out = xg[g][:].rearrange("p r t -> p (r t)").bitcast(F32).rearrange("p (a r u) -> p a r u", a=RT, u=2)
-            for pair in range(2):
+            if True:
                 tr = bank("tr_%d_%d" % (g, pair), [P, 2, 2, P], F32, "B%d" % ((2 * g + pair) % 4))
                 for a in range(2):
                     words = src[:, 2 * pair + a, :].bitcast(F32)
@@ -244,12 +246,16 @@ def tile_slstmcell_pb_kernel(tc, x, h_prev, c, n, W_o, b_o, U_o, out_0, out_1):
         interleave(1, 1, 0)
         quant_w(1, 0)
         quant_w(1, 1)
-        turn_x(0)
-        turn_x(1)
-        turn_x(2)
+        turn_x(0, 0)
+        turn_x(1, 0)
+        turn_x(0, 1)
+        turn_x(1, 1)
         quant_x(0)
         quant_x(1)
-        turn_x(3, on_vector=True)
+        turn_x(2, 0)
+        turn_x(3, 0, on_vector=True)
+        turn_x(2, 1)
+        turn_x(3, 1, on_vector=True)
         mx(0, 0)
         mx(0, 1)
         mx(1, 0)

@@ -264,7 +264,7 @@ def tile_slstmcell_pb_kernel(tc, x, h_prev, c, n, W_o, b_o, U_o, out_0, out_1):
         quant_x(2)
         quant_x(3)
         interleave(2, 0, 0)
-        interleave(2, 1, HALF)
+        interleave(2, 1, 256)
         nc.scalar.activation(out=warm[:, 1:2], in_=one[:], func=ACT.Sigmoid)
         quant_w(2, 0)
         mx(0, 2)

from contextlib import ExitStack

import concourse.mybir as mybir
from concourse.masks import make_identity

B, D_IN, D_H = 512, 1024, 1024
FLOPS = 2 * B * (D_IN + D_H) * D_H

F32 = mybir.dt.float32
BF16 = mybir.dt.bfloat16
U32 = mybir.dt.uint32
U8 = mybir.dt.uint8
FP8X4 = mybir.dt.float8_e4m3fn_x4
FP8 = mybir.dt.float8_e4m3fn
ACT = mybir.ActivationFunctionType
ALU = mybir.AluOpType
AX = mybir.AxisListType

P = 128
RT = B // P
NPASS = 4
HALF = 512
HROW = D_H + 8


def tile_slstmcell_pb_kernel(tc, x, h_prev, c, n, W_o, b_o, U_o, out_0, out_1):
    nc = tc.nc
    with ExitStack() as ctx:
        keep = ctx.enter_context(tc.tile_pool(name="keep", bufs=1))
        wgp = ctx.enter_context(tc.tile_pool(name="wgp", bufs=4))
        psum = ctx.enter_context(tc.psum_pool(name="psum", bufs=1))
        ctx.enter_context(tc.manual_schedule())

        def bank(name, shape, dtype, tag):
            return psum.tile(shape, dtype, name=name, tag=tag)

        w_raw = [keep.tile([P, 4, D_H], BF16, name="w_raw_%d" % g) for g in range(NPASS)]
        x_sb = [keep.tile([P, RT, 1024], BF16, name="x_sb"), keep.tile([P, RT, 1024], BF16, name="h_sb")]
        n_sb = keep.tile([P, RT, D_H], BF16, name="n_sb")
        c_sb = keep.tile([P, RT, D_H], BF16, name="c_sb")
        wq = keep.tile([P, NPASS, D_H], U32, name="wq", align_bytes=64)
        ws = keep.tile([P, NPASS, D_H], U8, name="ws", align_bytes=64)
        xq = keep.tile([P, NPASS, B], U32, name="xq", align_bytes=64)
        xs = keep.tile([P, NPASS, B], U8, name="xs", align_bytes=64)
        xg = [keep.tile([P, B, 4], BF16, name="xg_%d" % g, align_bytes=64) for g in range(NPASS)]
        rq = keep.tile([P, RT, D_H], F32, name="rq")
        h_all = keep.tile([P, RT, HROW], F32, name="h_all")
        am = keep.tile([P, RT], F32, name="am")
        ra = keep.tile([P, RT], F32, name="ra")
        sc = keep.tile([P, RT], F32, name="sc")
        o8 = [keep.tile([P, D_H], FP8, name="o8_%d" % t) for t in range(RT)]
        ot = {}
        for s in range(2):
            for k in range(4):
                ot[(s, k)] = keep.tile([P, B], F32, name="ot_%d_%d" % (s, k))
        ident = keep.tile([P, P], F32, name="ident")
        identb = keep.tile([P, P], BF16, name="identb")
        b_rows = keep.tile([P, P], BF16, name="b_rows")
        b_sb = keep.tile([P, 8], F32, name="b_sb")
        zero = keep.tile([P, 1], F32, name="zero")
        one = keep.tile([P, 1], F32, name="one")
        warm = keep.tile([P, 2], F32, name="warm")
        hold = keep.tile([P, 1], F32, name="hold")
        oc = keep.tile([P, HALF], F32, name="oc")

        out0_v = out_0.rearrange("(p t) m -> p t m", t=RT)
        out1_v = out_1.rearrange("(p t) m -> p t m", t=RT)

        def load_w(g):
            src = W_o if g < 2 else U_o
            k0 = 512 * (g % 2)
            nc.sync.dma_start(out=w_raw[g][:], in_=src[k0 : k0 + 512, :].rearrange("(p j) m -> p j m", j=4))

        def load_rows(dst, src, t0, t1):
            nc.sync.dma_start(out=dst[:, t0:t1, :], in_=src.rearrange("(p t) k -> p t k", t=RT)[:, t0:t1, :])

        load_w(0)
        load_rows(n_sb, n, 0, 2)
        load_w(1)
        load_rows(x_sb[0], x, 0, 2)
        load_rows(x_sb[0], x, 2, 4)
        load_rows(x_sb[1], h_prev, 0, 2)
        load_rows(x_sb[1], h_prev, 2, 4)
        load_rows(n_sb, n, 2, 4)
        load_w(2)
        load_w(3)
        load_rows(c_sb, c, 0, 4)

        nc.gpsimd.memset(b_rows[:], 0.0)
        make_identity(nc, identb[:])
        make_identity(nc, ident[:])
        nc.vector.memset(one[:], 1.0)
        nc.vector.memset(zero[:], 0.0)
        nc.scalar.dma_start(out=b_rows[0:8, :], in_=b_o.rearrange("(t p) -> t p", p=P))
        nc.scalar.activation(out=warm[:, 0:1], in_=one[:], func=ACT.Abs_reciprocal_sqrt)
        b_t = bank("b_t", [P, P], BF16, "A3")
        nc.tensor.transpose(b_t[:], b_rows[:], identb[:])

        wg = {}

        def interleave_part(g, s, lo, hi):
            if lo == 0:
                wg[(g, s)] = wgp.tile([P, HALF, 4], BF16, name="wg_%d_%d" % (g, s), tag="wg", align_bytes=64)
            nc.vector.tensor_copy(
                out=wg[(g, s)][:, lo:hi, :].rearrange("p (q i) j -> p q j i", i=4),
                in_=w_raw[g][:, :, HALF * s + lo : HALF * s + hi].rearrange("p j (q i) -> p q j i", i=4),
            )

        def quant_part(g, s, lo, hi):
            cols = slice(HALF * s + lo, HALF * s + hi)
            nc.vector.quantize_mx(
                out=wq[:, g, cols].bitcast(FP8X4), scales=ws[:, g, cols], in_=wg[(g, s)][:, lo:hi, :].rearrange("p m j -> p (m j)")
            )

        def interleave(g, s, s_cols):
            t = wgp.tile([P, HALF, 4], BF16, name="wg_%d_%d" % (g, s), tag="wg", align_bytes=64)
            wg[(g, s)] = t
            a = HALF - s_cols
            src = w_raw[g][:, :, HALF * s : HALF * (s + 1)]
            if a > 0:
                nc.vector.tensor_copy(
                    out=t[:, 0:a, :].rearrange("p (q i) j -> p q j i", i=4), in_=src[:, :, 0:a].rearrange("p j (q i) -> p q j i", i=4)
                )
            if s_cols > 0:
                nc.scalar.copy(
                    out=t[:, a:HALF, :].rearrange("p (q i) j -> p q j i", i=4),
                    in_=src[:, :, a:HALF].rearrange("p j (q i) -> p q j i", i=4),
                )

        def quant_w(g, s):
            cols = slice(HALF * s, HALF * (s + 1))
            nc.vector.quantize_mx(
                out=wq[:, g, cols].bitcast(FP8X4), scales=ws[:, g, cols], in_=wg[(g, s)][:].rearrange("p m j -> p (m j)")
            )

        def rsqrt_n(t0, t1):
            nc.scalar.activation(out=rq[:, t0:t1, :], in_=n_sb[:, t0:t1, :], func=ACT.Abs_reciprocal_sqrt, bias=1e-6, scale=1.0)

        def square_n(t):
            nc.scalar.activation(out=rq[:, t, :], in_=rq[:, t, :], func=ACT.Square)

        def ratio(eng, t, s):
            cols = slice(HALF * s, HALF * (s + 1))
            eng.tensor_tensor(out=rq[:, t, cols], in0=c_sb[:, t, cols], in1=rq[:, t, cols], op=ALU.mult)

        def turn_x(g, pair, on_vector=False):
            src = x_sb[g // 2]
            gl = g % 2
            words_out = xg[g][:].rearrange("p r t -> p (r t)").bitcast(F32).rearrange("p (a r u) -> p a r u", a=RT, u=2)
            if True:
                tr = bank("tr_%d_%d" % (g, pair), [P, 2, 2, P], F32, "B%d" % ((2 * g + pair) % 4))
                for a in range(2):
                    words = src[:, 2 * pair + a, :].bitcast(F32)
                    for u in range(2):
                        nc.tensor.transpose(tr[:, a, u, :], words[:, 256 * gl + u : 256 * (gl + 1) : 2], ident[:])
                if on_vector:
                    nc.vector.tensor_copy(out=words_out[:, 2 * pair : 2 * pair + 2, :, :], in_=tr[:].rearrange("p a u r -> p a r u"))
                else:
                    nc.scalar.copy(out=words_out[:, 2 * pair : 2 * pair + 2, :, :], in_=tr[:].rearrange("p a u r -> p a r u"))

        def quant_x(g):
            nc.vector.quantize_mx(out=xq[:, g, :].bitcast(FP8X4), scales=xs[:, g, :], in_=xg[g][:].rearrange("p r t -> p (r t)"))

        acc = {}

        def mx(s, g):
            for k in range(4):
                if g == 0:
                    acc[(s, k)] = bank("acc_%d_%d" % (s, k), [P, B], F32, "%s%d" % ("AB"[s], k))
                ch = slice(HALF * s + P * k, HALF * s + P * (k + 1))
                nc.tensor.matmul_mx(
                    out=acc[(s, k)][:],
                    lhsT=wq[:, g, ch].bitcast(FP8X4),
                    lhsT_scale=ws[:, g, ch],
                    rhs=xq[:, g, :].bitcast(FP8X4),
                    rhs_scale=xs[:, g, :],
                    start=(g == 0),
                    stop=(g == NPASS - 1),
                )

        def gate(s):
            for k in range(4):
                nc.scalar.activation(
                    out=ot[(s, k)][:], in_=acc[(s, k)][:], func=ACT.Sigmoid, bias=b_sb[:, 4 * s + k : 4 * s + k + 1], scale=1.0
                )

        ob = {}

        def back(s, t):
            ob[(s, t)] = bank("ob_%d_%d" % (s, t), [P, HALF], F32, "%s%d" % ("AB"[s], t))
            for k in range(4):
                nc.tensor.transpose(ob[(s, t)][:, P * k : P * (k + 1)], ot[(s, k)][:, P * t : P * (t + 1)], ident[:])

        def prod(s, t):
            cols = slice(HALF * s, HALF * (s + 1))
            nc.vector.tensor_tensor(out=h_all[:, t, cols], in0=ob[(s, t)][:], in1=rq[:, t, cols], op=ALU.mult)
            nc.sync.dma_start(out=out0_v[:, t, cols], in_=h_all[:, t, cols])

        def o_copy(s, t):
            nc.scalar.copy(out=oc[:], in_=ob[(s, t)][:])

        def prod_g(s, t):
            cols = slice(HALF * s, HALF * (s + 1))
            nc.gpsimd.tensor_tensor(out=h_all[:, t, cols], in0=oc[:], in1=rq[:, t, cols], op=ALU.mult)
            nc.sync.dma_start(out=out0_v[:, t, cols], in_=h_all[:, t, cols])

        def amax(s, t):
            if s == 0:
                nc.vector.tensor_reduce(
                    out=h_all[:, t, D_H : D_H + 1], in_=h_all[:, t, 0:HALF], axis=AX.X, op=ALU.max, apply_absolute_value=True
                )
            else:
                nc.vector.tensor_reduce(
                    out=am[:, t : t + 1], in_=h_all[:, t, HALF : D_H + 1], axis=AX.X, op=ALU.max, apply_absolute_value=True
                )

        def recip(t):
            nc.vector.reciprocal(out=ra[:, t : t + 1], in_=am[:, t : t + 1])

        def cast_s(t, v_cols):
            nc.scalar.activation(out=sc[:, t : t + 1], in_=ra[:, t : t + 1], func=ACT.Copy, scale=448.0)
            a = D_H - v_cols
            nc.scalar.activation(
                out=o8[t][:, 0:a], in_=h_all[:, t, 0:a], func=ACT.Identity, scale=sc[:, t : t + 1], bias=zero[:, 0:1], saturate=False
            )

        def cast_v(t, v_cols):
            a = D_H - v_cols
            nc.vector.tensor_scalar(
                out=o8[t][:, a:D_H], in0=h_all[:, t, a:D_H], scalar1=sc[:, t : t + 1], scalar2=None, op0=ALU.mult, saturate=False
            )

        def store8(t):
            nc.sync.dma_start(out=out1_v[:, t, :], in_=o8[t][:].bitcast(U8))

        interleave(0, 0, 0)
        interleave(0, 1, 256)
        quant_w(0, 0)
        quant_w(0, 1)
        rsqrt_n(0, 1)
        rsqrt_n(1, 2)
        square_n(0)
        square_n(1)
        nc.scalar.copy(out=b_sb[:], in_=b_t[:, 0:8])
        interleave(1, 0, 0)
        interleave(1, 1, 0)
        quant_w(1, 0)
        quant_w(1, 1)
        turn_x(0, 0)
        turn_x(1, 0)
        turn_x(0, 1)
        turn_x(1, 1)
        quant_x(0)
        quant_x(1)
        turn_x(2, 0)
        turn_x(3, 0, on_vector=True)
        turn_x(2, 1)
        turn_x(3, 1, on_vector=True)
        mx(0, 0)
        mx(0, 1)
        mx(1, 0)
        mx(1, 1)
        rsqrt_n(2, 4)
        quant_x(2)
        quant_x(3)
        interleave(2, 0, 0)
        interleave(2, 1, 256)
        nc.scalar.activation(out=warm[:, 1:2], in_=one[:], func=ACT.Sigmoid)
        quant_w(2, 0)
        mx(0, 2)
        interleave_part(3, 0, 0, 128)
        interleave_part(3, 0, 128, 256)
        quant_part(3, 0, 0, 128)
        interleave_part(3, 0, 256, 384)
        quant_part(3, 0, 128, 256)
        interleave_part(3, 0, 384, HALF)
        quant_part(3, 0, 256, 384)
        quant_part(3, 0, 384, HALF)
        mx(0, 3)
        quant_w(2, 1)
        mx(1, 2)
        interleave(3, 1, 0)
        ratio(nc.vector, 0, 0)
        quant_w(3, 1)
        ratio(nc.vector, 1, 0)
        ratio(nc.vector, 0, 1)
        gate(0)
        square_n(2)
        nc.gpsimd.tensor_copy(out=hold[:], in_=rq[:, 0, HALF : HALF + 1])
        ratio(nc.gpsimd, 2, 0)
        ratio(nc.gpsimd, 1, 1)
        ratio(nc.gpsimd, 2, 1)
        back(0, 0)
        back(0, 1)
        mx(1, 3)
        back(0, 2)
        prod(0, 0)
        prod(0, 1)
        amax(0, 0)
        amax(0, 1)
        gate(1)
        square_n(3)
        ratio(nc.gpsimd, 3, 0)
        ratio(nc.gpsimd, 3, 1)
        back(1, 0)
        back(1, 1)
        back(1, 2)
        back(0, 3)
        back(1, 3)
        o_copy(1, 3)
        prod(0, 2)
        prod(1, 0)
        amax(0, 2)
        prod(1, 1)
        amax(1, 0)
        prod(1, 2)
        recip(0)
        cast_s(0, 0)
        store8(0)
        amax(1, 1)
        prod(0, 3)
        recip(1)
        cast_s(1, 0)
        store8(1)
        amax(1, 2)
        prod_g(1, 3)
        amax(0, 3)
        recip(2)
        cast_s(2, 512)
        amax(1, 3)
        cast_v(2, 512)
        store8(2)
        recip(3)
        cast_s(3, 640)
        cast_v(3, 640)
        store8(3)
